import numpy as np
import ml_dtypes


def mxq(x, axis, fmt="e4m3"):
    dtype, down = {"e4m3": (ml_dtypes.float8_e4m3fn, 7), "e5m2": (ml_dtypes.float8_e5m2, 14)}[fmt]
    v = np.moveaxis(np.asarray(x, np.float32).astype(ml_dtypes.bfloat16).astype(np.float64), axis, -1)
    blocks = v.reshape(v.shape[:-1] + (-1, 32))
    amax = np.abs(blocks).max(-1, keepdims=True)
    byte = np.maximum(np.where(amax > 0, np.frexp(amax)[1] - 1 + 127, 0) - down, 1)
    scale = np.exp2(byte - 127.0)
    codes = (blocks / scale).astype(np.float32).astype(dtype).astype(np.float64)
    return np.moveaxis((codes * scale).reshape(v.shape), -1, axis)


WIDE = False


def mx_kscale(k):
    if not WIDE:
        return np.ones(k)
    levels = np.array([10, -10, 5, -5, 0])
    a = np.random.permutation(np.resize(levels, k // 512 * 4)).reshape(k // 512, 4)
    idx = np.arange(k)
    return np.exp2(a[idx // 512, idx % 128 // 32])


BF16 = ml_dtypes.bfloat16


def bf(x):
    return np.asarray(x, np.float32).astype(BF16)


def f64(x):
    return np.asarray(x).astype(np.float64)


E2M1 = np.array([0.0, 0.5, 1.0, 1.5, 2.0, 3.0, 4.0, 6.0, -0.0, -0.5, -1.0, -1.5, -2.0, -3.0, -4.0, -6.0])


def pack_weight(w, fmt):
    k, n = w.shape
    w = f64(bf(w)).reshape(k // 32, 32, n)
    amax = np.abs(w).max(1)
    if fmt == "e4m3":
        byte = np.frexp(amax)[1] - 1 + 127 - 7
    else:
        mant, ex = np.frexp(amax / 6.0)
        byte = np.where(mant > 0.5, ex, ex - 1) + 127
    byte = np.clip(np.where(amax > 0, byte, 1), 1, 254)
    scaled = (w * np.exp2(127.0 - byte)[:, None, :]).reshape(k, n).astype(np.float32)
    by_word = np.ascontiguousarray(scaled.reshape(k // 512, 128, 4, n).transpose(0, 1, 3, 2))
    if fmt == "e4m3":
        words = by_word.astype(ml_dtypes.float8_e4m3fn).view(np.uint8)
    else:
        c = by_word.astype(ml_dtypes.float4_e2m1fn).view(np.uint8) & 0xF
        words = c[..., 0::2] | (c[..., 1::2] << 4)
    return np.ascontiguousarray(words), np.ascontiguousarray(byte.astype(np.uint8).reshape(k // 512, 16, n))


def unpack_weight(words, scales, fmt):
    g, p, n, _ = words.shape
    if fmt == "e4m3":
        vals = np.ascontiguousarray(words).view(ml_dtypes.float8_e4m3fn).astype(np.float64)
    else:
        nib = np.empty((g, p, n, 4), np.uint8)
        nib[..., 0::2] = words & 0xF
        nib[..., 1::2] = words >> 4
        vals = E2M1[nib]
    vals = vals * np.repeat(np.exp2(scales.astype(np.float64) - 127.0), 8, axis=1)[..., None]
    return vals.transpose(0, 1, 3, 2).reshape(g * 512, n)


B, N, K, D, L = 1, 128, 1, 4096, 5632


def setup_inputs():
    s = mx_kscale(D)
    limit = np.sqrt(6.0 / (D + L))
    lone = np.random.random((B, N, 1)) < 0.125
    a = (0.3 + 0.7 * np.random.random((B, N, K + 1))) * np.where(lone, 0.4 / (K + 1), 1.0)
    targets = bf(np.random.standard_normal((B, N, D)) * s)
    neighbors = bf(np.random.standard_normal((B, N, K, D)) * s)
    words, scales = pack_weight(np.random.uniform(-limit, limit, (D, L)) / s[:, None], "e4m3")
    return {"targets": targets,
            "neighbors": neighbors,
            "a": bf(a),
            "kernel_words": words,
            "kernel_scales": scales}


def reference(targets, neighbors, a, kernel_words, kernel_scales):
    neighborhood = np.concatenate([f64(targets)[..., None, :], f64(neighbors)], axis=-2)
    y = (mxq(neighborhood, 3, "e4m3") @ unpack_weight(kernel_words, kernel_scales, "e4m3")).sum(axis=-2)
    factor = f64(a).sum(axis=-1, keepdims=True)
    factor = np.where(factor > 0.5, factor, np.ones_like(factor))
    y = y / factor
    return np.maximum(y, 0.0)

@@ -1,0 +1,156 @@
+from contextlib import ExitStack
+
+import concourse.mybir as mybir
+from concourse.masks import make_identity
+
+FLOPS = 2 * 2 * 128 * 4096 * 5632
+
+F32 = mybir.dt.float32
+BF16 = mybir.dt.bfloat16
+I32 = mybir.dt.int32
+U32 = mybir.dt.uint32
+U8 = mybir.dt.uint8
+FP8X4 = mybir.dt.float8_e4m3fn_x4
+ALU = mybir.AluOpType
+ACT = mybir.ActivationFunctionType
+
+P = 128
+D = 4096
+L = 5632
+G = 8
+CH = 512
+SCALES_ON_GPSIMD = False
+W_BUFS = 9
+ROUNDS = [(0, 6), (6, 11)]
+STORE_GROUPS = [(0, 3), (3, 6), (6, 9), (9, 11)]
+
+
+def tile_singlegcnlayer_w_kernel(tc, targets, neighbors, a, kernel_words, kernel_scales, out):
+    nc = tc.nc
+    x_dram = [targets.rearrange("b n d -> (b n) d"), neighbors.rearrange("b n k d -> (b n k) d")]
+    out2 = out.rearrange("b n l -> (b n) l")
+    with ExitStack() as ctx:
+        keep = ctx.enter_context(tc.tile_pool(name="keep", bufs=1))
+        gpool = ctx.enter_context(tc.tile_pool(name="gpool", bufs=4))
+        wpool = ctx.enter_context(tc.tile_pool(name="wpool", bufs=W_BUFS))
+        psum = ctx.enter_context(tc.psum_pool(name="psum", bufs=1))
+
+        planes = keep.tile([P, 2, L], U8, align_bytes=64)
+        for h in range(2):
+            nc.vector.memset(planes[:, h, :].bitcast(I32), 0)
+        warm_in = keep.tile([P, 1], F32)
+        warm_out = keep.tile([P, 1], F32)
+        nc.vector.memset(warm_in[:], 0.0)
+        nc.scalar.copy(out=warm_out[:], in_=warm_in[:])
+        ident = keep.tile([P, P], F32)
+        make_identity(nc, ident[:])
+
+        a_sb = keep.tile([P, 2], BF16)
+        nc.scalar.dma_start(out=a_sb[:], in_=a.rearrange("b n k -> (b n) k"))
+
+        x_sb = {}
+        for hf in range(2):
+            for m in range(2):
+                xt = keep.tile([P, D // 2], BF16, name="x_%d_%d" % (m, hf))
+                nc.sync.dma_start(out=xt[:], in_=x_dram[m][:, hf * (D // 2) : (hf + 1) * (D // 2)])
+                x_sb[(m, hf)] = xt
+
+        def load_planes(h):
+            for q in range(4):
+                dst = planes[32 * q : 32 * q + 16, h, :]
+                src = kernel_scales[4 * h : 4 * h + 4, 4 * q : 4 * q + 4, :]
+                if SCALES_ON_GPSIMD:
+                    nc.gpsimd.dma_start(out=dst.bitcast(F32), in_=src.bitcast(F32))
+                else:
+                    nc.sync.dma_start(out=dst.bitcast(I32), in_=src.bitcast(I32))
+
+        load_planes(0)
+        if SCALES_ON_GPSIMD:
+            load_planes(1)
+
+        a32 = keep.tile([P, 2], F32)
+        nc.vector.tensor_copy(out=a32[:], in_=a_sb[:])
+        deg = keep.tile([P, 1], F32)
+        nc.vector.tensor_tensor(out=deg[:], in0=a32[:, 0:1], in1=a32[:, 1:2], op=ALU.add)
+        big = keep.tile([P, 1], F32)
+        nc.vector.tensor_single_scalar(out=big[:], in_=deg[:], scalar=0.5, op=ALU.is_gt)
+        kept = keep.tile([P, 1], F32)
+        nc.vector.tensor_tensor(out=kept[:], in0=deg[:], in1=big[:], op=ALU.mult)
+        small = keep.tile([P, 1], F32)
+        nc.vector.tensor_scalar(out=small[:], in0=big[:], scalar1=-1.0, scalar2=1.0, op0=ALU.mult, op1=ALU.add)
+        factor = keep.tile([P, 1], F32)
+        nc.vector.tensor_tensor(out=factor[:], in0=kept[:], in1=small[:], op=ALU.max)
+        recip = keep.tile([P, 1], F32)
+        nc.vector.reciprocal(out=recip[:], in_=factor[:])
+
+        codes = keep.tile([P, 2, G, P], U32, align_bytes=64)
+        xpl = keep.tile([P, 2, G, P], U8, align_bytes=64)
+        bank_no = 0
+        for hf in range(2):
+            for m in range(2):
+                xw = x_sb[(m, hf)][:].bitcast(F32)
+                grouped = gpool.tile([P, 4, P, 4], BF16, align_bytes=64)
+                for pair in range(2):
+                    bank = psum.tile([P, 2, 2, P], F32, name="tp_%d" % bank_no, tag="bank%d" % bank_no)
+                    for gg in range(2):
+                        gl = 2 * pair + gg
+                        for u in range(2):
+                            nc.tensor.transpose(bank[:, gg, u, :], xw[:, 256 * gl + u : 256 * (gl + 1) : 2], ident[:])
+                    dst = grouped[:, 2 * pair : 2 * pair + 2, :, :].bitcast(F32)
+                    src = bank[:].rearrange("p g u r -> p g r u")
+                    if pair == 0:
+                        nc.scalar.copy(out=dst, in_=src)
+                    else:
+                        nc.vector.tensor_copy(out=dst, in_=src)
+                    bank_no += 1
+                g0 = 4 * hf
+                nc.vector.quantize_mx(
+                    out=codes[:, m, g0 : g0 + 4, :].rearrange("p g r -> p (g r)").bitcast(FP8X4),
+                    scales=xpl[:, m, g0 : g0 + 4, :].rearrange("p g r -> p (g r)"),
+                    in_=grouped[:].rearrange("p g r t -> p (g r t)"),
+                )
+
+        o_tiles = {}
+        for (s0, s1) in STORE_GROUPS:
+            ot = keep.tile([P, (s1 - s0) * CH], F32, name="o_%d" % s0)
+            for c in range(s0, s1):
+                o_tiles[c] = (ot, s0, s1)
+
+        for rnd, (c0, c1) in enumerate(ROUNDS):
+            acc = {}
+            for c in range(c0, c1):
+                acc[c] = psum.tile([P, CH], F32, name="acc_%d" % c, tag="bank%d" % (c % 8))
+            for g in range(G):
+                if rnd == 0 and g == 0:
+                    cuts = [(0, 3), (3, 6)]
+                elif rnd == len(ROUNDS) - 1 and g == G - 1:
+                    cuts = [(6, 9), (9, 11)]
+                else:
+                    cuts = [(c0, c1)]
+                for (p0, p1) in cuts:
+                    wt = wpool.tile([P, 6 * CH], U32, tag="w", align_bytes=64)
+                    n = (p1 - p0) * CH
+                    src = kernel_words[g].rearrange("p n t -> p (n t)")[:, 4 * p0 * CH : 4 * p1 * CH].bitcast(I32)
+                    nc.sync.dma_start(out=wt[:, 0:n].bitcast(I32), in_=src)
+                    for c in range(p0, p1):
+                        for m in range(2):
+                            nc.tensor.matmul_mx(
+                                out=acc[c][:],
+                                lhsT=codes[:, m, g, :].bitcast(FP8X4),
+                                lhsT_scale=xpl[:, m, g, :],
+                                rhs=wt[:, (c - p0) * CH : (c - p0 + 1) * CH].bitcast(FP8X4),
+                                rhs_scale=planes[4 * (g % 4) : P, g // 4, c * CH : (c + 1) * CH],
+                                start=(g == 0 and m == 0),
+                                stop=(g == G - 1 and m == 1),
+                            )
+                if rnd == 0 and g == 1 and not SCALES_ON_GPSIMD:
+                    load_planes(1)
+            for c in range(c0, c1):
+                ot, s0, s1 = o_tiles[c]
+                dst = ot[:, (c - s0) * CH : (c - s0 + 1) * CH]
+                if c % 2 == 0:
+                    nc.scalar.activation(out=dst, in_=acc[c][:], func=ACT.Relu, scale=recip[:, 0:1])
+                else:
+                    nc.vector.tensor_scalar(out=dst, in0=acc[c][:], scalar1=recip[:, 0:1], scalar2=0.0, op0=ALU.mult, op1=ALU.max)
+                if c == s1 - 1:
+                    nc.sync.dma_start(out=out2[:, s0 * CH : s1 * CH], in_=ot[:])

@@ -19,7 +19,7 @@ D = 4096
 L = 5632
 G = 8
 CH = 512
-SCALES_ON_GPSIMD = False
+SCALES_ON_GPSIMD = True
 W_BUFS = 9
 ROUNDS = [(0, 6), (6, 11)]
 STORE_GROUPS = [(0, 3), (3, 6), (6, 9), (9, 11)]

@@ -19,10 +19,13 @@ D = 4096
 L = 5632
 G = 8
 CH = 512
-SCALES_ON_GPSIMD = True
+PINNED = True
 W_BUFS = 9
 ROUNDS = [(0, 6), (6, 11)]
-STORE_GROUPS = [(0, 3), (3, 6), (6, 9), (9, 11)]
+FIRST_CUTS = [(0, 1), (1, 3), (3, 6)]
+LAST_CUTS = [(6, 9), (9, 11)]
+STORE_GROUPS = [(0, 6), (6, 9), (9, 11)]
+DEFERRED = [(0, 6)]
 
 
 def tile_singlegcnlayer_w_kernel(tc, targets, neighbors, a, kernel_words, kernel_scales, out):
@@ -34,10 +37,14 @@ def tile_singlegcnlayer_w_kernel(tc, targets, neighbors, a, kernel_words, kernel
         gpool = ctx.enter_context(tc.tile_pool(name="gpool", bufs=4))
         wpool = ctx.enter_context(tc.tile_pool(name="wpool", bufs=W_BUFS))
         psum = ctx.enter_context(tc.psum_pool(name="psum", bufs=1))
+        if PINNED:
+            ctx.enter_context(tc.manual_schedule())
 
-        planes = keep.tile([P, 2, L], U8, align_bytes=64)
+        planes = []
         for h in range(2):
-            nc.vector.memset(planes[:, h, :].bitcast(I32), 0)
+            pl = keep.tile([P, L], U8, name="planes_%d" % h, align_bytes=64)
+            nc.vector.memset(pl[:].bitcast(I32), 0)
+            planes.append(pl)
         warm_in = keep.tile([P, 1], F32)
         warm_out = keep.tile([P, 1], F32)
         nc.vector.memset(warm_in[:], 0.0)
@@ -55,33 +62,11 @@ def tile_singlegcnlayer_w_kernel(tc, targets, neighbors, a, kernel_words, kernel
                 nc.sync.dma_start(out=xt[:], in_=x_dram[m][:, hf * (D // 2) : (hf + 1) * (D // 2)])
                 x_sb[(m, hf)] = xt
 
-        def load_planes(h):
+        for h in range(2):
             for q in range(4):
-                dst = planes[32 * q : 32 * q + 16, h, :]
+                dst = planes[h][32 * q : 32 * q + 16, :]
                 src = kernel_scales[4 * h : 4 * h + 4, 4 * q : 4 * q + 4, :]
-                if SCALES_ON_GPSIMD:
-                    nc.gpsimd.dma_start(out=dst.bitcast(F32), in_=src.bitcast(F32))
-                else:
-                    nc.sync.dma_start(out=dst.bitcast(I32), in_=src.bitcast(I32))
-
-        load_planes(0)
-        if SCALES_ON_GPSIMD:
-            load_planes(1)
-
-        a32 = keep.tile([P, 2], F32)
-        nc.vector.tensor_copy(out=a32[:], in_=a_sb[:])
-        deg = keep.tile([P, 1], F32)
-        nc.vector.tensor_tensor(out=deg[:], in0=a32[:, 0:1], in1=a32[:, 1:2], op=ALU.add)
-        big = keep.tile([P, 1], F32)
-        nc.vector.tensor_single_scalar(out=big[:], in_=deg[:], scalar=0.5, op=ALU.is_gt)
-        kept = keep.tile([P, 1], F32)
-        nc.vector.tensor_tensor(out=kept[:], in0=deg[:], in1=big[:], op=ALU.mult)
-        small = keep.tile([P, 1], F32)
-        nc.vector.tensor_scalar(out=small[:], in0=big[:], scalar1=-1.0, scalar2=1.0, op0=ALU.mult, op1=ALU.add)
-        factor = keep.tile([P, 1], F32)
-        nc.vector.tensor_tensor(out=factor[:], in0=kept[:], in1=small[:], op=ALU.max)
-        recip = keep.tile([P, 1], F32)
-        nc.vector.reciprocal(out=recip[:], in_=factor[:])
+                nc.gpsimd.dma_start(out=dst.bitcast(F32), in_=src.bitcast(F32))
 
         codes = keep.tile([P, 2, G, P], U32, align_bytes=64)
         xpl = keep.tile([P, 2, G, P], U8, align_bytes=64)
@@ -110,21 +95,40 @@ def tile_singlegcnlayer_w_kernel(tc, targets, neighbors, a, kernel_words, kernel
                     in_=grouped[:].rearrange("p g r t -> p (g r t)"),
                 )
 
+        a32 = keep.tile([P, 2], F32)
+        nc.vector.tensor_copy(out=a32[:], in_=a_sb[:])
+        deg = keep.tile([P, 1], F32)
+        nc.vector.tensor_tensor(out=deg[:], in0=a32[:, 0:1], in1=a32[:, 1:2], op=ALU.add)
+        big = keep.tile([P, 1], F32)
+        nc.vector.tensor_single_scalar(out=big[:], in_=deg[:], scalar=0.5, op=ALU.is_gt)
+        kept = keep.tile([P, 1], F32)
+        nc.vector.tensor_tensor(out=kept[:], in0=deg[:], in1=big[:], op=ALU.mult)
+        small = keep.tile([P, 1], F32)
+        nc.vector.tensor_scalar(out=small[:], in0=big[:], scalar1=-1.0, scalar2=1.0, op0=ALU.mult, op1=ALU.add)
+        factor = keep.tile([P, 1], F32)
+        nc.vector.tensor_tensor(out=factor[:], in0=kept[:], in1=small[:], op=ALU.max)
+        recip = keep.tile([P, 1], F32)
+        nc.vector.reciprocal(out=recip[:], in_=factor[:])
+
         o_tiles = {}
         for (s0, s1) in STORE_GROUPS:
             ot = keep.tile([P, (s1 - s0) * CH], F32, name="o_%d" % s0)
             for c in range(s0, s1):
                 o_tiles[c] = (ot, s0, s1)
 
+        def store(s0, s1):
+            nc.sync.dma_start(out=out2[:, s0 * CH : s1 * CH], in_=o_tiles[s0][0][:])
+
         for rnd, (c0, c1) in enumerate(ROUNDS):
+            last_round = rnd == len(ROUNDS) - 1
             acc = {}
             for c in range(c0, c1):
                 acc[c] = psum.tile([P, CH], F32, name="acc_%d" % c, tag="bank%d" % (c % 8))
             for g in range(G):
                 if rnd == 0 and g == 0:
-                    cuts = [(0, 3), (3, 6)]
-                elif rnd == len(ROUNDS) - 1 and g == G - 1:
-                    cuts = [(6, 9), (9, 11)]
+                    cuts = FIRST_CUTS
+                elif last_round and g == G - 1:
+                    cuts = LAST_CUTS
                 else:
                     cuts = [(c0, c1)]
                 for (p0, p1) in cuts:
@@ -132,6 +136,9 @@ def tile_singlegcnlayer_w_kernel(tc, targets, neighbors, a, kernel_words, kernel
                     n = (p1 - p0) * CH
                     src = kernel_words[g].rearrange("p n t -> p (n t)")[:, 4 * p0 * CH : 4 * p1 * CH].bitcast(I32)
                     nc.sync.dma_start(out=wt[:, 0:n].bitcast(I32), in_=src)
+                    if last_round and g == G - 1 and (p0, p1) == cuts[-1]:
+                        for (s0, s1) in DEFERRED:
+                            store(s0, s1)
                     for c in range(p0, p1):
                         for m in range(2):
                             nc.tensor.matmul_mx(
@@ -139,12 +146,10 @@ def tile_singlegcnlayer_w_kernel(tc, targets, neighbors, a, kernel_words, kernel
                                 lhsT=codes[:, m, g, :].bitcast(FP8X4),
                                 lhsT_scale=xpl[:, m, g, :],
                                 rhs=wt[:, (c - p0) * CH : (c - p0 + 1) * CH].bitcast(FP8X4),
-                                rhs_scale=planes[4 * (g % 4) : P, g // 4, c * CH : (c + 1) * CH],
+                                rhs_scale=planes[g // 4][4 * (g % 4) : P, c * CH : (c + 1) * CH],
                                 start=(g == 0 and m == 0),
                                 stop=(g == G - 1 and m == 1),
                             )
-                if rnd == 0 and g == 1 and not SCALES_ON_GPSIMD:
-                    load_planes(1)
             for c in range(c0, c1):
                 ot, s0, s1 = o_tiles[c]
                 dst = ot[:, (c - s0) * CH : (c - s0 + 1) * CH]
@@ -152,5 +157,5 @@ def tile_singlegcnlayer_w_kernel(tc, targets, neighbors, a, kernel_words, kernel
                     nc.scalar.activation(out=dst, in_=acc[c][:], func=ACT.Relu, scale=recip[:, 0:1])
                 else:
                     nc.vector.tensor_scalar(out=dst, in0=acc[c][:], scalar1=recip[:, 0:1], scalar2=0.0, op0=ALU.mult, op1=ALU.max)
-                if c == s1 - 1:
-                    nc.sync.dma_start(out=out2[:, s0 * CH : s1 * CH], in_=ot[:])
+                if c == s1 - 1 and (s0, s1) not in DEFERRED:
+                    store(s0, s1)

@@ -40,11 +40,12 @@ def tile_singlegcnlayer_w_kernel(tc, targets, neighbors, a, kernel_words, kernel
         if PINNED:
             ctx.enter_context(tc.manual_schedule())
 
-        planes = []
-        for h in range(2):
-            pl = keep.tile([P, L], U8, name="planes_%d" % h, align_bytes=64)
-            nc.vector.memset(pl[:].bitcast(I32), 0)
-            planes.append(pl)
+        planes = {}
+        for rnd, (c0, c1) in enumerate(ROUNDS):
+            for h in range(2):
+                pl = keep.tile([P, (c1 - c0) * CH], U8, name="planes_%d_%d" % (rnd, h), align_bytes=64)
+                nc.vector.memset(pl[:].bitcast(I32), 0)
+                planes[(rnd, h)] = pl
         warm_in = keep.tile([P, 1], F32)
         warm_out = keep.tile([P, 1], F32)
         nc.vector.memset(warm_in[:], 0.0)
@@ -62,11 +63,15 @@ def tile_singlegcnlayer_w_kernel(tc, targets, neighbors, a, kernel_words, kernel
                 nc.sync.dma_start(out=xt[:], in_=x_dram[m][:, hf * (D // 2) : (hf + 1) * (D // 2)])
                 x_sb[(m, hf)] = xt
 
-        for h in range(2):
-            for q in range(4):
-                dst = planes[h][32 * q : 32 * q + 16, :]
-                src = kernel_scales[4 * h : 4 * h + 4, 4 * q : 4 * q + 4, :]
-                nc.gpsimd.dma_start(out=dst.bitcast(F32), in_=src.bitcast(F32))
+        for rnd, (c0, c1) in enumerate(ROUNDS):
+            for h in range(2):
+                for q in range(4):
+                    dst = planes[(rnd, h)][32 * q : 32 * q + 16, :]
+                    src = kernel_scales[4 * h : 4 * h + 4, 4 * q : 4 * q + 4, c0 * CH : c1 * CH]
+                    if rnd == 0 and h == 0:
+                        nc.sync.dma_start(out=dst.bitcast(I32), in_=src.bitcast(I32))
+                    else:
+                        nc.gpsimd.dma_start(out=dst.bitcast(F32), in_=src.bitcast(F32))
 
         codes = keep.tile([P, 2, G, P], U32, align_bytes=64)
         xpl = keep.tile([P, 2, G, P], U8, align_bytes=64)
@@ -146,7 +151,7 @@ def tile_singlegcnlayer_w_kernel(tc, targets, neighbors, a, kernel_words, kernel
                                 lhsT=codes[:, m, g, :].bitcast(FP8X4),
                                 lhsT_scale=xpl[:, m, g, :],
                                 rhs=wt[:, (c - p0) * CH : (c - p0 + 1) * CH].bitcast(FP8X4),
-                                rhs_scale=planes[g // 4][4 * (g % 4) : P, c * CH : (c + 1) * CH],
+                                rhs_scale=planes[(rnd, g // 4)][4 * (g % 4) : P, (c - c0) * CH : (c - c0 + 1) * CH],
                                 start=(g == 0 and m == 0),
                                 stop=(g == G - 1 and m == 1),
                             )

@@ -23,8 +23,8 @@ PINNED = True
 W_BUFS = 9
 ROUNDS = [(0, 6), (6, 11)]
 FIRST_CUTS = [(0, 1), (1, 3), (3, 6)]
-LAST_CUTS = [(6, 9), (9, 11)]
-STORE_GROUPS = [(0, 6), (6, 9), (9, 11)]
+LAST_CUTS = [(6, 9), (9, 10), (10, 11)]
+STORE_GROUPS = [(0, 6), (6, 9), (9, 10), (10, 11)]
 DEFERRED = [(0, 6)]
 
 
@@ -40,16 +40,15 @@ def tile_singlegcnlayer_w_kernel(tc, targets, neighbors, a, kernel_words, kernel
         if PINNED:
             ctx.enter_context(tc.manual_schedule())
 
-        planes = {}
-        for rnd, (c0, c1) in enumerate(ROUNDS):
-            for h in range(2):
-                pl = keep.tile([P, (c1 - c0) * CH], U8, name="planes_%d_%d" % (rnd, h), align_bytes=64)
-                nc.vector.memset(pl[:].bitcast(I32), 0)
-                planes[(rnd, h)] = pl
         warm_in = keep.tile([P, 1], F32)
         warm_out = keep.tile([P, 1], F32)
         nc.vector.memset(warm_in[:], 0.0)
         nc.scalar.copy(out=warm_out[:], in_=warm_in[:])
+        planes = []
+        for h in range(2):
+            pl = keep.tile([P, L], U8, name="planes_%d" % h, align_bytes=64)
+            nc.vector.memset(pl[:].bitcast(I32), 0)
+            planes.append(pl)
         ident = keep.tile([P, P], F32)
         make_identity(nc, ident[:])
 
@@ -63,15 +62,15 @@ def tile_singlegcnlayer_w_kernel(tc, targets, neighbors, a, kernel_words, kernel
                 nc.sync.dma_start(out=xt[:], in_=x_dram[m][:, hf * (D // 2) : (hf + 1) * (D // 2)])
                 x_sb[(m, hf)] = xt
 
-        for rnd, (c0, c1) in enumerate(ROUNDS):
-            for h in range(2):
-                for q in range(4):
-                    dst = planes[(rnd, h)][32 * q : 32 * q + 16, :]
-                    src = kernel_scales[4 * h : 4 * h + 4, 4 * q : 4 * q + 4, c0 * CH : c1 * CH]
-                    if rnd == 0 and h == 0:
-                        nc.sync.dma_start(out=dst.bitcast(I32), in_=src.bitcast(I32))
-                    else:
-                        nc.gpsimd.dma_start(out=dst.bitcast(F32), in_=src.bitcast(F32))
+        held = []
+        for h in range(2):
+            for q in range(4):
+                dst = planes[h][32 * q : 32 * q + 16, :]
+                src = kernel_scales[4 * h : 4 * h + 4, 4 * q : 4 * q + 4, :]
+                nc.gpsimd.dma_start(out=dst.bitcast(F32), in_=src.bitcast(F32))
+            hw = wpool.tile([P, 6 * CH], U32, name="w_held_%d" % h, tag="w", align_bytes=64)
+            nc.gpsimd.memset(hw[:, 0:1].bitcast(F32), 0.0)
+            held.append(hw)
 
         codes = keep.tile([P, 2, G, P], U32, align_bytes=64)
         xpl = keep.tile([P, 2, G, P], U8, align_bytes=64)
@@ -137,7 +136,10 @@ def tile_singlegcnlayer_w_kernel(tc, targets, neighbors, a, kernel_words, kernel
                 else:
                     cuts = [(c0, c1)]
                 for (p0, p1) in cuts:
-                    wt = wpool.tile([P, 6 * CH], U32, tag="w", align_bytes=64)
+                    if rnd == 0 and g < 2 and (p0, p1) == cuts[0]:
+                        wt = held[g]
+                    else:
+                        wt = wpool.tile([P, 6 * CH], U32, tag="w", align_bytes=64)
                     n = (p1 - p0) * CH
                     src = kernel_words[g].rearrange("p n t -> p (n t)")[:, 4 * p0 * CH : 4 * p1 * CH].bitcast(I32)
                     nc.sync.dma_start(out=wt[:, 0:n].bitcast(I32), in_=src)
@@ -151,7 +153,7 @@ def tile_singlegcnlayer_w_kernel(tc, targets, neighbors, a, kernel_words, kernel
                                 lhsT=codes[:, m, g, :].bitcast(FP8X4),
                                 lhsT_scale=xpl[:, m, g, :],
                                 rhs=wt[:, (c - p0) * CH : (c - p0 + 1) * CH].bitcast(FP8X4),
-                                rhs_scale=planes[(rnd, g // 4)][4 * (g % 4) : P, (c - c0) * CH : (c - c0 + 1) * CH],
+                                rhs_scale=planes[g // 4][4 * (g % 4) : P, c * CH : (c + 1) * CH],
                                 start=(g == 0 and m == 0),
                                 stop=(g == G - 1 and m == 1),
                             )

@@ -19,13 +19,14 @@ D = 4096
 L = 5632
 G = 8
 CH = 512
-PINNED = True
-W_BUFS = 9
+HALF = CH // 2
 ROUNDS = [(0, 6), (6, 11)]
 FIRST_CUTS = [(0, 1), (1, 3), (3, 6)]
+EARLY_CUTS = [(0, 3), (3, 6)]
 LAST_CUTS = [(6, 9), (9, 10), (10, 11)]
-STORE_GROUPS = [(0, 6), (6, 9), (9, 10), (10, 11)]
-DEFERRED = [(0, 6)]
+LAST_CHUNK = 10
+W_WIDTH = [3, 5]
+W_BUFS = [14, 6]
 
 
 def tile_singlegcnlayer_w_kernel(tc, targets, neighbors, a, kernel_words, kernel_scales, out):
@@ -35,10 +36,9 @@ def tile_singlegcnlayer_w_kernel(tc, targets, neighbors, a, kernel_words, kernel
     with ExitStack() as ctx:
         keep = ctx.enter_context(tc.tile_pool(name="keep", bufs=1))
         gpool = ctx.enter_context(tc.tile_pool(name="gpool", bufs=4))
-        wpool = ctx.enter_context(tc.tile_pool(name="wpool", bufs=W_BUFS))
+        wpools = [ctx.enter_context(tc.tile_pool(name="wpool%d" % r, bufs=W_BUFS[r])) for r in range(2)]
         psum = ctx.enter_context(tc.psum_pool(name="psum", bufs=1))
-        if PINNED:
-            ctx.enter_context(tc.manual_schedule())
+        ctx.enter_context(tc.manual_schedule())
 
         warm_in = keep.tile([P, 1], F32)
         warm_out = keep.tile([P, 1], F32)
@@ -68,7 +68,7 @@ def tile_singlegcnlayer_w_kernel(tc, targets, neighbors, a, kernel_words, kernel
                 dst = planes[h][32 * q : 32 * q + 16, :]
                 src = kernel_scales[4 * h : 4 * h + 4, 4 * q : 4 * q + 4, :]
                 nc.gpsimd.dma_start(out=dst.bitcast(F32), in_=src.bitcast(F32))
-            hw = wpool.tile([P, 6 * CH], U32, name="w_held_%d" % h, tag="w", align_bytes=64)
+            hw = wpools[0].tile([P, W_WIDTH[0] * CH], U32, name="w_held_%d" % h, tag="w0", align_bytes=64)
             nc.gpsimd.memset(hw[:, 0:1].bitcast(F32), 0.0)
             held.append(hw)
 
@@ -114,24 +114,30 @@ def tile_singlegcnlayer_w_kernel(tc, targets, neighbors, a, kernel_words, kernel
         recip = keep.tile([P, 1], F32)
         nc.vector.reciprocal(out=recip[:], in_=factor[:])
 
-        o_tiles = {}
-        for (s0, s1) in STORE_GROUPS:
-            ot = keep.tile([P, (s1 - s0) * CH], F32, name="o_%d" % s0)
-            for c in range(s0, s1):
-                o_tiles[c] = (ot, s0, s1)
+        def evacuate(on_scalar, dst, acc_ap):
+            if on_scalar:
+                nc.scalar.activation(out=dst, in_=acc_ap, func=ACT.Relu, scale=recip[:, 0:1])
+            else:
+                nc.vector.tensor_scalar(out=dst, in0=acc_ap, scalar1=recip[:, 0:1], scalar2=0.0, op0=ALU.mult, op1=ALU.max)
 
-        def store(s0, s1):
-            nc.sync.dma_start(out=out2[:, s0 * CH : s1 * CH], in_=o_tiles[s0][0][:])
-
+        o_first = keep.tile([P, 6 * CH], F32, name="o_first")
         for rnd, (c0, c1) in enumerate(ROUNDS):
             last_round = rnd == len(ROUNDS) - 1
-            acc = {}
+            groups = {}
             for c in range(c0, c1):
-                acc[c] = psum.tile([P, CH], F32, name="acc_%d" % c, tag="bank%d" % (c % 8))
+                if c == LAST_CHUNK:
+                    groups[c] = [
+                        (c * CH + i * HALF, HALF, psum.tile([P, HALF], F32, name="acc_%d_%d" % (c, i), tag="bank%d" % (c % 8 + i)))
+                        for i in range(2)
+                    ]
+                else:
+                    groups[c] = [(c * CH, CH, psum.tile([P, CH], F32, name="acc_%d" % c, tag="bank%d" % (c % 8)))]
             for g in range(G):
                 if rnd == 0 and g == 0:
                     cuts = FIRST_CUTS
-                elif last_round and g == G - 1:
+                elif rnd == 0:
+                    cuts = EARLY_CUTS
+                elif g == G - 1:
                     cuts = LAST_CUTS
                 else:
                     cuts = [(c0, c1)]
@@ -139,30 +145,34 @@ def tile_singlegcnlayer_w_kernel(tc, targets, neighbors, a, kernel_words, kernel
                     if rnd == 0 and g < 2 and (p0, p1) == cuts[0]:
                         wt = held[g]
                     else:
-                        wt = wpool.tile([P, 6 * CH], U32, tag="w", align_bytes=64)
+                        wt = wpools[rnd].tile([P, W_WIDTH[rnd] * CH], U32, name="w_%d" % rnd, tag="w%d" % rnd, align_bytes=64)
                     n = (p1 - p0) * CH
                     src = kernel_words[g].rearrange("p n t -> p (n t)")[:, 4 * p0 * CH : 4 * p1 * CH].bitcast(I32)
                     nc.sync.dma_start(out=wt[:, 0:n].bitcast(I32), in_=src)
                     if last_round and g == G - 1 and (p0, p1) == cuts[-1]:
-                        for (s0, s1) in DEFERRED:
-                            store(s0, s1)
-                    for c in range(p0, p1):
-                        for m in range(2):
-                            nc.tensor.matmul_mx(
-                                out=acc[c][:],
-                                lhsT=codes[:, m, g, :].bitcast(FP8X4),
-                                lhsT_scale=xpl[:, m, g, :],
-                                rhs=wt[:, (c - p0) * CH : (c - p0 + 1) * CH].bitcast(FP8X4),
-                                rhs_scale=planes[g // 4][4 * (g % 4) : P, c * CH : (c + 1) * CH],
-                                start=(g == 0 and m == 0),
-                                stop=(g == G - 1 and m == 1),
-                            )
-            for c in range(c0, c1):
-                ot, s0, s1 = o_tiles[c]
-                dst = ot[:, (c - s0) * CH : (c - s0 + 1) * CH]
-                if c % 2 == 0:
-                    nc.scalar.activation(out=dst, in_=acc[c][:], func=ACT.Relu, scale=recip[:, 0:1])
-                else:
-                    nc.vector.tensor_scalar(out=dst, in0=acc[c][:], scalar1=recip[:, 0:1], scalar2=0.0, op0=ALU.mult, op1=ALU.max)
-                if c == s1 - 1 and (s0, s1) not in DEFERRED:
-                    store(s0, s1)
+                        nc.sync.dma_start(out=out2[:, 0 : 6 * CH], in_=o_first[:])
+                    for m in range(2):
+                        for c in range(p0, p1):
+                            for (col0, width, acc) in groups[c]:
+                                nc.tensor.matmul_mx(
+                                    out=acc[:],
+                                    lhsT=codes[:, m, g, :].bitcast(FP8X4),
+                                    lhsT_scale=xpl[:, m, g, :],
+                                    rhs=wt[:, col0 - p0 * CH : col0 - p0 * CH + width].bitcast(FP8X4),
+                                    rhs_scale=planes[g // 4][4 * (g % 4) : P, col0 : col0 + width],
+                                    start=(g == 0 and m == 0),
+                                    stop=(g == G - 1 and m == 1),
+                                )
+            if not last_round:
+                for c in range(c0, c1):
+                    evacuate(c % 2 == 0, o_first[:, c * CH : (c + 1) * CH], groups[c][0][2][:])
+            else:
+                o_mid = keep.tile([P, 3 * CH], F32, name="o_mid")
+                for c in range(6, 9):
+                    evacuate(c % 2 == 0, o_mid[:, (c - 6) * CH : (c - 5) * CH], groups[c][0][2][:])
+                nc.sync.dma_start(out=out2[:, 6 * CH : 9 * CH], in_=o_mid[:])
+                for (on_scalar, (col0, width, acc)) in zip((False, False, True), groups[9] + groups[10]):
+                    ot = keep.tile([P, width], F32, name="o_%d" % col0)
+                    evacuate(on_scalar, ot[:], acc[:])
+                    queue = nc.scalar if on_scalar else nc.sync
+                    queue.dma_start(out=out2[:, col0 : col0 + width], in_=ot[:])

@@ -40,17 +40,25 @@ def tile_singlegcnlayer_w_kernel(tc, targets, neighbors, a, kernel_words, kernel
         psum = ctx.enter_context(tc.psum_pool(name="psum", bufs=1))
         ctx.enter_context(tc.manual_schedule())
 
+        zero = keep.tile([P, CH], BF16)
+        nc.vector.memset(zero[:], 0.0)
         warm_in = keep.tile([P, 1], F32)
         warm_out = keep.tile([P, 1], F32)
         nc.vector.memset(warm_in[:], 0.0)
         nc.scalar.copy(out=warm_out[:], in_=warm_in[:])
+        ident = keep.tile([P, P], F32)
+        nc.vector.memset(ident[:], 0.0)
         planes = []
         for h in range(2):
             pl = keep.tile([P, L], U8, name="planes_%d" % h, align_bytes=64)
             nc.vector.memset(pl[:].bitcast(I32), 0)
             planes.append(pl)
-        ident = keep.tile([P, P], F32)
-        make_identity(nc, ident[:])
+        make_identity(nc, ident[:], nomemset=True)
+
+        def warm(n):
+            dummy = psum.tile([P, CH], F32, name="dummy", tag="bank7")
+            for i in range(n):
+                nc.tensor.matmul(dummy[:], lhsT=zero[:, 0:P], rhs=zero[:], start=True, stop=True)
 
         a_sb = keep.tile([P, 2], BF16)
         nc.scalar.dma_start(out=a_sb[:], in_=a.rearrange("b n k -> (b n) k"))
@@ -75,8 +83,11 @@ def tile_singlegcnlayer_w_kernel(tc, targets, neighbors, a, kernel_words, kernel
         codes = keep.tile([P, 2, G, P], U32, align_bytes=64)
         xpl = keep.tile([P, 2, G, P], U8, align_bytes=64)
         bank_no = 0
+        warm(5)
         for hf in range(2):
             for m in range(2):
+                if bank_no > 0:
+                    warm(2)
                 xw = x_sb[(m, hf)][:].bitcast(F32)
                 grouped = gpool.tile([P, 4, P, 4], BF16, align_bytes=64)
                 for pair in range(2):

@@ -23,7 +23,7 @@ HALF = CH // 2
 ROUNDS = [(0, 6), (6, 11)]
 FIRST_CUTS = [(0, 1), (1, 3), (3, 6)]
 EARLY_CUTS = [(0, 3), (3, 6)]
-LAST_CUTS = [(6, 9), (9, 10), (10, 11)]
+LAST_CUTS = [(6, 8), (8, 10), (10, 11)]
 LAST_CHUNK = 10
 W_WIDTH = [3, 5]
 W_BUFS = [14, 6]
@@ -162,27 +162,30 @@ def tile_singlegcnlayer_w_kernel(tc, targets, neighbors, a, kernel_words, kernel
                     nc.sync.dma_start(out=wt[:, 0:n].bitcast(I32), in_=src)
                     if last_round and g == G - 1 and (p0, p1) == cuts[-1]:
                         nc.sync.dma_start(out=out2[:, 0 : 6 * CH], in_=o_first[:])
-                    for m in range(2):
-                        for c in range(p0, p1):
-                            for (col0, width, acc) in groups[c]:
-                                nc.tensor.matmul_mx(
-                                    out=acc[:],
-                                    lhsT=codes[:, m, g, :].bitcast(FP8X4),
-                                    lhsT_scale=xpl[:, m, g, :],
-                                    rhs=wt[:, col0 - p0 * CH : col0 - p0 * CH + width].bitcast(FP8X4),
-                                    rhs_scale=planes[g // 4][4 * (g % 4) : P, col0 : col0 + width],
-                                    start=(g == 0 and m == 0),
-                                    stop=(g == G - 1 and m == 1),
-                                )
+                    order = [(m, grp) for m in range(2) for c in range(p0, p1) for grp in groups[c]]
+                    if last_round and g == G - 1:
+                        order = [(m, grp) for c in range(p0, p1) for grp in groups[c] for m in range(2)]
+                    for (m, (col0, width, acc)) in order:
+                        nc.tensor.matmul_mx(
+                            out=acc[:],
+                            lhsT=codes[:, m, g, :].bitcast(FP8X4),
+                            lhsT_scale=xpl[:, m, g, :],
+                            rhs=wt[:, col0 - p0 * CH : col0 - p0 * CH + width].bitcast(FP8X4),
+                            rhs_scale=planes[g // 4][4 * (g % 4) : P, col0 : col0 + width],
+                            start=(g == 0 and m == 0),
+                            stop=(g == G - 1 and m == 1),
+                        )
             if not last_round:
                 for c in range(c0, c1):
                     evacuate(c % 2 == 0, o_first[:, c * CH : (c + 1) * CH], groups[c][0][2][:])
             else:
-                o_mid = keep.tile([P, 3 * CH], F32, name="o_mid")
-                for c in range(6, 9):
-                    evacuate(c % 2 == 0, o_mid[:, (c - 6) * CH : (c - 5) * CH], groups[c][0][2][:])
-                nc.sync.dma_start(out=out2[:, 6 * CH : 9 * CH], in_=o_mid[:])
-                for (on_scalar, (col0, width, acc)) in zip((False, False, True), groups[9] + groups[10]):
+                for (p0, p1) in LAST_CUTS[:-1]:
+                    ot = keep.tile([P, 2 * CH], F32, name="o_%d" % p0)
+                    for c in range(p0, p1):
+                        evacuate(c % 2 == 1, ot[:, (c - p0) * CH : (c - p0 + 1) * CH], groups[c][0][2][:])
+                    nc.sync.dma_start(out=out2[:, p0 * CH : p1 * CH], in_=ot[:])
+                for i, (col0, width, acc) in enumerate(groups[LAST_CHUNK]):
+                    on_scalar = i == 1
                     ot = keep.tile([P, width], F32, name="o_%d" % col0)
                     evacuate(on_scalar, ot[:], acc[:])
                     queue = nc.scalar if on_scalar else nc.sync

@@ -23,7 +23,8 @@ HALF = CH // 2
 ROUNDS = [(0, 6), (6, 11)]
 FIRST_CUTS = [(0, 1), (1, 3), (3, 6)]
 EARLY_CUTS = [(0, 3), (3, 6)]
-LAST_CUTS = [(6, 8), (8, 10), (10, 11)]
+LAST_CUTS = [(6, 9), (9, 11)]
+STORE_CUTS = [(6, 8), (8, 10)]
 LAST_CHUNK = 10
 W_WIDTH = [3, 5]
 W_BUFS = [14, 6]
@@ -40,6 +41,11 @@ def tile_singlegcnlayer_w_kernel(tc, targets, neighbors, a, kernel_words, kernel
         psum = ctx.enter_context(tc.psum_pool(name="psum", bufs=1))
         ctx.enter_context(tc.manual_schedule())
 
+        planes = []
+        for h in range(2):
+            pl = keep.tile([P, L], U8, name="planes_%d" % h, align_bytes=64)
+            planes.append(pl)
+        nc.vector.memset(planes[0][:].bitcast(I32), 0)
         zero = keep.tile([P, CH], BF16)
         nc.vector.memset(zero[:], 0.0)
         warm_in = keep.tile([P, 1], F32)
@@ -48,12 +54,7 @@ def tile_singlegcnlayer_w_kernel(tc, targets, neighbors, a, kernel_words, kernel
         nc.scalar.copy(out=warm_out[:], in_=warm_in[:])
         ident = keep.tile([P, P], F32)
         nc.vector.memset(ident[:], 0.0)
-        planes = []
-        for h in range(2):
-            pl = keep.tile([P, L], U8, name="planes_%d" % h, align_bytes=64)
-            nc.vector.memset(pl[:].bitcast(I32), 0)
-            planes.append(pl)
-        make_identity(nc, ident[:], nomemset=True)
+        nc.vector.memset(planes[1][:].bitcast(I32), 0)
 
         def warm(n):
             dummy = psum.tile([P, CH], F32, name="dummy", tag="bank7")
@@ -64,11 +65,10 @@ def tile_singlegcnlayer_w_kernel(tc, targets, neighbors, a, kernel_words, kernel
         nc.scalar.dma_start(out=a_sb[:], in_=a.rearrange("b n k -> (b n) k"))
 
         x_sb = {}
-        for hf in range(2):
-            for m in range(2):
-                xt = keep.tile([P, D // 2], BF16, name="x_%d_%d" % (m, hf))
-                nc.sync.dma_start(out=xt[:], in_=x_dram[m][:, hf * (D // 2) : (hf + 1) * (D // 2)])
-                x_sb[(m, hf)] = xt
+        for m in range(2):
+            xt = keep.tile([P, D], BF16, name="x_%d" % m)
+            nc.sync.dma_start(out=xt[:], in_=x_dram[m])
+            x_sb[m] = xt
 
         held = []
         for h in range(2):
@@ -76,6 +76,8 @@ def tile_singlegcnlayer_w_kernel(tc, targets, neighbors, a, kernel_words, kernel
                 dst = planes[h][32 * q : 32 * q + 16, :]
                 src = kernel_scales[4 * h : 4 * h + 4, 4 * q : 4 * q + 4, :]
                 nc.gpsimd.dma_start(out=dst.bitcast(F32), in_=src.bitcast(F32))
+                if h == 0 and q == 1:
+                    make_identity(nc, ident[:], nomemset=True)
             hw = wpools[0].tile([P, W_WIDTH[0] * CH], U32, name="w_held_%d" % h, tag="w0", align_bytes=64)
             nc.gpsimd.memset(hw[:, 0:1].bitcast(F32), 0.0)
             held.append(hw)
@@ -84,11 +86,11 @@ def tile_singlegcnlayer_w_kernel(tc, targets, neighbors, a, kernel_words, kernel
         xpl = keep.tile([P, 2, G, P], U8, align_bytes=64)
         bank_no = 0
         warm(5)
-        for hf in range(2):
-            for m in range(2):
+        for m in range(2):
+            for hf in range(2):
                 if bank_no > 0:
                     warm(2)
-                xw = x_sb[(m, hf)][:].bitcast(F32)
+                xw = x_sb[m][:].bitcast(F32)[:, hf * (D // 4) : (hf + 1) * (D // 4)]
                 grouped = gpool.tile([P, 4, P, 4], BF16, align_bytes=64)
                 for pair in range(2):
                     bank = psum.tile([P, 2, 2, P], F32, name="tp_%d" % bank_no, tag="bank%d" % bank_no)
@@ -179,7 +181,7 @@ def tile_singlegcnlayer_w_kernel(tc, targets, neighbors, a, kernel_words, kernel
                 for c in range(c0, c1):
                     evacuate(c % 2 == 0, o_first[:, c * CH : (c + 1) * CH], groups[c][0][2][:])
             else:
-                for (p0, p1) in LAST_CUTS[:-1]:
+                for (p0, p1) in STORE_CUTS:
                     ot = keep.tile([P, 2 * CH], F32, name="o_%d" % p0)
                     for c in range(p0, p1):
                         evacuate(c % 2 == 1, ot[:, (c - p0) * CH : (c - p0 + 1) * CH], groups[c][0][2][:])

@@ -21,7 +21,6 @@ G = 8
 CH = 512
 HALF = CH // 2
 ROUNDS = [(0, 6), (6, 11)]
-FIRST_CUTS = [(0, 1), (1, 3), (3, 6)]
 EARLY_CUTS = [(0, 3), (3, 6)]
 LAST_CUTS = [(6, 9), (9, 11)]
 STORE_CUTS = [(6, 8), (8, 10)]
@@ -88,7 +87,7 @@ def tile_singlegcnlayer_w_kernel(tc, targets, neighbors, a, kernel_words, kernel
         warm(5)
         for m in range(2):
             for hf in range(2):
-                if bank_no > 0:
+                if bank_no in (2, 4):
                     warm(2)
                 xw = x_sb[m][:].bitcast(F32)[:, hf * (D // 4) : (hf + 1) * (D // 4)]
                 grouped = gpool.tile([P, 4, P, 4], BF16, align_bytes=64)
@@ -146,9 +145,7 @@ def tile_singlegcnlayer_w_kernel(tc, targets, neighbors, a, kernel_words, kernel
                 else:
                     groups[c] = [(c * CH, CH, psum.tile([P, CH], F32, name="acc_%d" % c, tag="bank%d" % (c % 8)))]
             for g in range(G):
-                if rnd == 0 and g == 0:
-                    cuts = FIRST_CUTS
-                elif rnd == 0:
+                if rnd == 0:
                     cuts = EARLY_CUTS
                 elif g == G - 1:
                     cuts = LAST_CUTS

@@ -53,7 +53,8 @@ def tile_singlegcnlayer_w_kernel(tc, targets, neighbors, a, kernel_words, kernel
         nc.scalar.copy(out=warm_out[:], in_=warm_in[:])
         ident = keep.tile([P, P], F32)
         nc.vector.memset(ident[:], 0.0)
-        nc.vector.memset(planes[1][:].bitcast(I32), 0)
+        nc.vector.memset(planes[1][:, 0 : L - 4].bitcast(I32), 0)
+        nc.vector.memset(planes[1][:, L - 4 : L].bitcast(I32), 0)
 
         def warm(n):
             dummy = psum.tile([P, CH], F32, name="dummy", tag="bank7")
@@ -86,30 +87,35 @@ def tile_singlegcnlayer_w_kernel(tc, targets, neighbors, a, kernel_words, kernel
         bank_no = 0
         warm(5)
         for m in range(2):
+            grouped = []
             for hf in range(2):
                 if bank_no in (2, 4):
                     warm(2)
                 xw = x_sb[m][:].bitcast(F32)[:, hf * (D // 4) : (hf + 1) * (D // 4)]
-                grouped = gpool.tile([P, 4, P, 4], BF16, align_bytes=64)
+                gt = gpool.tile([P, 4, P, 4], BF16, name="grouped", align_bytes=64)
+                grouped.append(gt)
                 for pair in range(2):
                     bank = psum.tile([P, 2, 2, P], F32, name="tp_%d" % bank_no, tag="bank%d" % bank_no)
                     for gg in range(2):
                         gl = 2 * pair + gg
                         for u in range(2):
                             nc.tensor.transpose(bank[:, gg, u, :], xw[:, 256 * gl + u : 256 * (gl + 1) : 2], ident[:])
-                    dst = grouped[:, 2 * pair : 2 * pair + 2, :, :].bitcast(F32)
+                    dst = gt[:, 2 * pair : 2 * pair + 2, :, :].bitcast(F32)
                     src = bank[:].rearrange("p g u r -> p g r u")
                     if pair == 0:
                         nc.scalar.copy(out=dst, in_=src)
                     else:
                         nc.vector.tensor_copy(out=dst, in_=src)
                     bank_no += 1
-                g0 = 4 * hf
-                nc.vector.quantize_mx(
-                    out=codes[:, m, g0 : g0 + 4, :].rearrange("p g r -> p (g r)").bitcast(FP8X4),
-                    scales=xpl[:, m, g0 : g0 + 4, :].rearrange("p g r -> p (g r)"),
-                    in_=grouped[:].rearrange("p g r t -> p (g r t)"),
-                )
+                if m == 0 and hf == 0:
+                    continue
+                for h in range(2) if m == 0 else [hf]:
+                    g0 = 4 * h
+                    nc.vector.quantize_mx(
+                        out=codes[:, m, g0 : g0 + 4, :].rearrange("p g r -> p (g r)").bitcast(FP8X4),
+                        scales=xpl[:, m, g0 : g0 + 4, :].rearrange("p g r -> p (g r)"),
+                        in_=grouped[h][:].rearrange("p g r t -> p (g r t)"),
+                    )
 
         a32 = keep.tile([P, 2], F32)
         nc.vector.tensor_copy(out=a32[:], in_=a_sb[:])

from contextlib import ExitStack

import concourse.mybir as mybir
from concourse.masks import make_identity

FLOPS = 2 * 2 * 128 * 4096 * 5632

F32 = mybir.dt.float32
BF16 = mybir.dt.bfloat16
I32 = mybir.dt.int32
U32 = mybir.dt.uint32
U8 = mybir.dt.uint8
FP8X4 = mybir.dt.float8_e4m3fn_x4
ALU = mybir.AluOpType
ACT = mybir.ActivationFunctionType

P = 128
D = 4096
L = 5632
G = 8
CH = 512
HALF = CH // 2
ROUNDS = [(0, 6), (6, 11)]
EARLY_CUTS = [(0, 3), (3, 6)]
LAST_CUTS = [(6, 9), (9, 11)]
STORE_CUTS = [(6, 8), (8, 10)]
LAST_CHUNK = 10
W_WIDTH = [3, 5]
W_BUFS = [14, 6]


def tile_singlegcnlayer_w_kernel(tc, targets, neighbors, a, kernel_words, kernel_scales, out):
    nc = tc.nc
    x_dram = [targets.rearrange("b n d -> (b n) d"), neighbors.rearrange("b n k d -> (b n k) d")]
    out2 = out.rearrange("b n l -> (b n) l")
    with ExitStack() as ctx:
        keep = ctx.enter_context(tc.tile_pool(name="keep", bufs=1))
        gpool = ctx.enter_context(tc.tile_pool(name="gpool", bufs=4))
        wpools = [ctx.enter_context(tc.tile_pool(name="wpool%d" % r, bufs=W_BUFS[r])) for r in range(2)]
        psum = ctx.enter_context(tc.psum_pool(name="psum", bufs=1))
        ctx.enter_context(tc.manual_schedule())

        planes = []
        for h in range(2):
            pl = keep.tile([P, L], U8, name="planes_%d" % h, align_bytes=64)
            planes.append(pl)
        nc.vector.memset(planes[0][:].bitcast(I32), 0)
        zero = keep.tile([P, CH], BF16)
        nc.vector.memset(zero[:], 0.0)
        warm_in = keep.tile([P, 1], F32)
        warm_out = keep.tile([P, 1], F32)
        nc.vector.memset(warm_in[:], 0.0)
        nc.scalar.copy(out=warm_out[:], in_=warm_in[:])
        ident = keep.tile([P, P], F32)
        nc.vector.memset(ident[:], 0.0)
        nc.vector.memset(planes[1][:, 0 : L - 4].bitcast(I32), 0)
        nc.vector.memset(planes[1][:, L - 4 : L].bitcast(I32), 0)

        def warm(n):
            dummy = psum.tile([P, CH], F32, name="dummy", tag="bank7")
            for i in range(n):
                nc.tensor.matmul(dummy[:], lhsT=zero[:, 0:P], rhs=zero[:], start=True, stop=True)

        a_sb = keep.tile([P, 2], BF16)
        nc.scalar.dma_start(out=a_sb[:], in_=a.rearrange("b n k -> (b n) k"))

        x_sb = {}
        for m in range(2):
            xt = keep.tile([P, D], BF16, name="x_%d" % m)
            nc.sync.dma_start(out=xt[:], in_=x_dram[m])
            x_sb[m] = xt

        held = []
        for h in range(2):
            for q in range(4):
                dst = planes[h][32 * q : 32 * q + 16, :]
                src = kernel_scales[4 * h : 4 * h + 4, 4 * q : 4 * q + 4, :]
                nc.gpsimd.dma_start(out=dst.bitcast(F32), in_=src.bitcast(F32))
                if h == 0 and q == 1:
                    make_identity(nc, ident[:], nomemset=True)
            hw = wpools[0].tile([P, W_WIDTH[0] * CH], U32, name="w_held_%d" % h, tag="w0", align_bytes=64)
            nc.gpsimd.memset(hw[:, 0:1].bitcast(F32), 0.0)
            held.append(hw)

        codes = keep.tile([P, 2, G, P], U32, align_bytes=64)
        xpl = keep.tile([P, 2, G, P], U8, align_bytes=64)
        bank_no = 0
        warm(5)
        for m in range(2):
            grouped = []
            for hf in range(2):
                if bank_no in (2, 4):
                    warm(2)
                xw = x_sb[m][:].bitcast(F32)[:, hf * (D // 4) : (hf + 1) * (D // 4)]
                gt = gpool.tile([P, 4, P, 4], BF16, name="grouped", align_bytes=64)
                grouped.append(gt)
                for pair in range(2):
                    bank = psum.tile([P, 2, 2, P], F32, name="tp_%d" % bank_no, tag="bank%d" % bank_no)
                    for gg in range(2):
                        gl = 2 * pair + gg
                        for u in range(2):
                            nc.tensor.transpose(bank[:, gg, u, :], xw[:, 256 * gl + u : 256 * (gl + 1) : 2], ident[:])
                    dst = gt[:, 2 * pair : 2 * pair + 2, :, :].bitcast(F32)
                    src = bank[:].rearrange("p g u r -> p g r u")
                    if pair == 0:
                        nc.scalar.copy(out=dst, in_=src)
                    else:
                        nc.vector.tensor_copy(out=dst, in_=src)
                    bank_no += 1
                if m == 0 and hf == 0:
                    continue
                for h in range(2) if m == 0 else [hf]:
                    g0 = 4 * h
                    nc.vector.quantize_mx(
                        out=codes[:, m, g0 : g0 + 4, :].rearrange("p g r -> p (g r)").bitcast(FP8X4),
                        scales=xpl[:, m, g0 : g0 + 4, :].rearrange("p g r -> p (g r)"),
                        in_=grouped[h][:].rearrange("p g r t -> p (g r t)"),
                    )

        a32 = keep.tile([P, 2], F32)
        nc.vector.tensor_copy(out=a32[:], in_=a_sb[:])
        deg = keep.tile([P, 1], F32)
        nc.vector.tensor_tensor(out=deg[:], in0=a32[:, 0:1], in1=a32[:, 1:2], op=ALU.add)
        big = keep.tile([P, 1], F32)
        nc.vector.tensor_single_scalar(out=big[:], in_=deg[:], scalar=0.5, op=ALU.is_gt)
        kept = keep.tile([P, 1], F32)
        nc.vector.tensor_tensor(out=kept[:], in0=deg[:], in1=big[:], op=ALU.mult)
        small = keep.tile([P, 1], F32)
        nc.vector.tensor_scalar(out=small[:], in0=big[:], scalar1=-1.0, scalar2=1.0, op0=ALU.mult, op1=ALU.add)
        factor = keep.tile([P, 1], F32)
        nc.vector.tensor_tensor(out=factor[:], in0=kept[:], in1=small[:], op=ALU.max)
        recip = keep.tile([P, 1], F32)
        nc.vector.reciprocal(out=recip[:], in_=factor[:])

        def evacuate(on_scalar, dst, acc_ap):
            if on_scalar:
                nc.scalar.activation(out=dst, in_=acc_ap, func=ACT.Relu, scale=recip[:, 0:1])
            else:
                nc.vector.tensor_scalar(out=dst, in0=acc_ap, scalar1=recip[:, 0:1], scalar2=0.0, op0=ALU.mult, op1=ALU.max)

        o_first = keep.tile([P, 6 * CH], F32, name="o_first")
        for rnd, (c0, c1) in enumerate(ROUNDS):
            last_round = rnd == len(ROUNDS) - 1
            groups = {}
            for c in range(c0, c1):
                if c == LAST_CHUNK:
                    groups[c] = [
                        (c * CH + i * HALF, HALF, psum.tile([P, HALF], F32, name="acc_%d_%d" % (c, i), tag="bank%d" % (c % 8 + i)))
                        for i in range(2)
                    ]
                else:
                    groups[c] = [(c * CH, CH, psum.tile([P, CH], F32, name="acc_%d" % c, tag="bank%d" % (c % 8)))]
            for g in range(G):
                if rnd == 0:
                    cuts = EARLY_CUTS
                elif g == G - 1:
                    cuts = LAST_CUTS
                else:
                    cuts = [(c0, c1)]
                for (p0, p1) in cuts:
                    if rnd == 0 and g < 2 and (p0, p1) == cuts[0]:
                        wt = held[g]
                    else:
                        wt = wpools[rnd].tile([P, W_WIDTH[rnd] * CH], U32, name="w_%d" % rnd, tag="w%d" % rnd, align_bytes=64)
                    n = (p1 - p0) * CH
                    src = kernel_words[g].rearrange("p n t -> p (n t)")[:, 4 * p0 * CH : 4 * p1 * CH].bitcast(I32)
                    nc.sync.dma_start(out=wt[:, 0:n].bitcast(I32), in_=src)
                    if last_round and g == G - 1 and (p0, p1) == cuts[-1]:
                        nc.sync.dma_start(out=out2[:, 0 : 6 * CH], in_=o_first[:])
                    order = [(m, grp) for m in range(2) for c in range(p0, p1) for grp in groups[c]]
                    if last_round and g == G - 1:
                        order = [(m, grp) for c in range(p0, p1) for grp in groups[c] for m in range(2)]
                    for (m, (col0, width, acc)) in order:
                        nc.tensor.matmul_mx(
                            out=acc[:],
                            lhsT=codes[:, m, g, :].bitcast(FP8X4),
                            lhsT_scale=xpl[:, m, g, :],
                            rhs=wt[:, col0 - p0 * CH : col0 - p0 * CH + width].bitcast(FP8X4),
                            rhs_scale=planes[g // 4][4 * (g % 4) : P, col0 : col0 + width],
                            start=(g == 0 and m == 0),
                            stop=(g == G - 1 and m == 1),
                        )
            if not last_round:
                for c in range(c0, c1):
                    evacuate(c % 2 == 0, o_first[:, c * CH : (c + 1) * CH], groups[c][0][2][:])
            else:
                for (p0, p1) in STORE_CUTS:
                    ot = keep.tile([P, 2 * CH], F32, name="o_%d" % p0)
                    for c in range(p0, p1):
                        evacuate(c % 2 == 1, ot[:, (c - p0) * CH : (c - p0 + 1) * CH], groups[c][0][2][:])
                    nc.sync.dma_start(out=out2[:, p0 * CH : p1 * CH], in_=ot[:])
                for i, (col0, width, acc) in enumerate(groups[LAST_CHUNK]):
                    on_scalar = i == 1
                    ot = keep.tile([P, width], F32, name="o_%d" % col0)
                    evacuate(on_scalar, ot[:], acc[:])
                    queue = nc.scalar if on_scalar else nc.sync
                    queue.dma_start(out=out2[:, col0 : col0 + width], in_=ot[:])
